import numpy as np
import ml_dtypes


def mxq(x, axis, fmt="e4m3"):
    dtype, down = {"e4m3": (ml_dtypes.float8_e4m3fn, 7), "e5m2": (ml_dtypes.float8_e5m2, 14)}[fmt]
    v = np.moveaxis(np.asarray(x, np.float32).astype(ml_dtypes.bfloat16).astype(np.float64), axis, -1)
    blocks = v.reshape(v.shape[:-1] + (-1, 32))
    amax = np.abs(blocks).max(-1, keepdims=True)
    byte = np.maximum(np.where(amax > 0, np.frexp(amax)[1] - 1 + 127, 0) - down, 1)
    scale = np.exp2(byte - 127.0)
    codes = (blocks / scale).astype(np.float32).astype(dtype).astype(np.float64)
    return np.moveaxis((codes * scale).reshape(v.shape), -1, axis)


WIDE = False


def mx_kscale(k):
    if not WIDE:
        return np.ones(k)
    levels = np.array([10, -10, 5, -5, 0])
    a = np.random.permutation(np.resize(levels, k // 512 * 4)).reshape(k // 512, 4)
    idx = np.arange(k)
    return np.exp2(a[idx // 512, idx % 128 // 32])


BF16 = ml_dtypes.bfloat16


def bf(x):
    return np.asarray(x, np.float32).astype(BF16)


def f64(x):
    return np.asarray(x).astype(np.float64)


B, K, F, INCH, OUTCH, R = 2, 8, 256, 1024, 1024, 128


def erf(a):
    c = np.clip(a, -6.0, 6.0)
    c2 = 2.0 * c * c
    t = c.copy()
    s = c.copy()
    n = 1.0
    while np.max(np.abs(t) - 1e-18 * np.abs(s)) > 0.0:
        n += 2.0
        t = t * c2 / n
        s = s + t
    return 2.0 / np.sqrt(np.pi) * np.exp(-c * c) * s


def gelu(t):
    return 0.5 * t * (1.0 + erf(t / np.sqrt(2.0)))


def setup_inputs():
    s = mx_kscale(INCH)
    return {
        "h": bf(gelu(np.random.standard_normal((B, K, F, INCH))) * s),
        "z": bf(np.random.standard_normal((B, K, F, R)) * 0.35),
        "u": bf(np.random.standard_normal((B, K, OUTCH, R)) * 1.5 * np.sqrt(R)),
        "b": bf(np.random.standard_normal((B, 1, 1, OUTCH)) * 0.3),
        "W_out": bf(np.random.standard_normal((OUTCH, INCH)) * 1.5 / np.sqrt(INCH) / s),
        "b_out": bf(np.random.standard_normal(OUTCH) * 0.3),
    }


def reference(h, z, u, b, W_out, b_out):
    lora = f64(z) @ f64(u).transpose(0, 1, 3, 2) / R
    main = mxq(f64(h), 3, "e4m3") @ mxq(f64(W_out).T, 0, "e4m3")
    return gelu(main + f64(b_out) + lora + f64(b))

@@ -1,0 +1,254 @@
+from contextlib import ExitStack
+
+import concourse.mybir as mybir
+from concourse.masks import make_identity
+
+F32 = mybir.dt.float32
+BF16 = mybir.dt.bfloat16
+U32 = mybir.dt.uint32
+U8 = mybir.dt.uint8
+FP8X4 = mybir.dt.float8_e4m3fn_x4
+ACTF = mybir.ActivationFunctionType
+ALU = mybir.AluOpType
+
+FLOPS = 2 * 4096 * 1024 * 1024 + 2 * 4096 * 1024 * 128
+
+P = 128
+UNITS = 16
+LOOKAHEAD_LOADS = 6
+ACT_P1 = (3,)
+MANUAL = True
+
+
+def tile_loratacmlp4_pb_t_kernel(tc, h, z, u, b, W_out, b_out, out):
+    nc = tc.nc
+    h_v = h.rearrange("a k (p t) c -> (a k) p (t c)", t=2)
+    z_v = z.rearrange("a k (p t) r -> p (a k) (t r)", t=2)
+    u_v = u.rearrange("a k (c p j) r -> (a k) p c (j r)", c=4, j=2)
+    w_v = W_out.rearrange("(c p j) k -> c p (j k)", c=4, j=2)
+    o_v = out.rearrange("a k (p t) o -> (a k) p t o", t=2)
+    b_v = b.rearrange("a x y o -> (x y) a o")
+    bo_v = b_out.rearrange("(x o) -> x o", x=1)
+
+    with ExitStack() as ctx:
+        const = ctx.enter_context(tc.tile_pool(name="const", bufs=1))
+        hpool = ctx.enter_context(tc.tile_pool(name="hpool", bufs=8))
+        upool = ctx.enter_context(tc.tile_pool(name="upool", bufs=8))
+        work = ctx.enter_context(tc.tile_pool(name="work", bufs=3))
+        prep = ctx.enter_context(tc.tile_pool(name="prep", bufs=3))
+        stg = ctx.enter_context(tc.tile_pool(name="stg", bufs=6))
+        psum = ctx.enter_context(tc.psum_pool(name="psum", bufs=8))
+        if MANUAL:
+            ctx.enter_context(tc.manual_schedule())
+
+        def bank(shape, dtype, name):
+            return psum.tile(shape, dtype, name=name, tag="ps")
+
+        ident_f = const.tile([P, P], F32, name="ident_f")
+        ident_b = const.tile([P, P], BF16, name="ident_b")
+        make_identity(nc, ident_b[:])
+        make_identity(nc, ident_f[:])
+        ones = const.tile([P, P], BF16, name="ones")
+        nc.vector.memset(ones[:], 1.0)
+        bias_in = const.tile([P, 2, 1024], BF16, name="bias_in")
+        nc.vector.memset(bias_in[:], 0.0)
+        warm = const.tile([P, 1], F32, name="warm")
+        nc.vector.memset(warm[:], 0.0)
+        nc.scalar.activation(out=warm[:], in_=warm[:], func=ACTF.Gelu)
+        nc.scalar.dma_start(out=bias_in[1:2, :, :], in_=b_v)
+        for a in range(2):
+            nc.scalar.dma_start(out=bias_in[0:1, a, :], in_=bo_v)
+
+        z_sb = [const.tile([P, 4, 256], BF16, name="z_sb%d" % k) for k in range(4)]
+        zT = [const.tile([P, 1024], BF16, name="zT%d" % k) for k in range(4)]
+        w_sb = [const.tile([P, 2048], BF16, name="w_sb%d" % c) for c in range(4)]
+        gW = [const.tile([P, 4096], BF16, name="gW%d" % n, align_bytes=64) for n in range(2)]
+        cW = [const.tile([P, 1024], U32, name="cW%d" % n, align_bytes=64) for n in range(2)]
+        sW = [const.tile([P, 1024], U8, name="sW%d" % n, align_bytes=64) for n in range(2)]
+        bias_sb = [const.tile([P, 1024], F32, name="bias_sb%d" % a) for a in range(2)]
+
+        h_sb, u_sb, hq, ch, sh, uT, pre, lo_ps, mx_ps, h_ps, u_ps = {}, {}, {}, {}, {}, {}, {}, {}, {}, {}, {}
+
+        def load_z(k):
+            nc.sync.dma_start(out=z_sb[k][:], in_=z_v[:, 4 * k : 4 * k + 4, :])
+
+        def load_w(c):
+            nc.sync.dma_start(out=w_sb[c][:], in_=w_v[c])
+
+        def load_u(i):
+            u_sb[i] = upool.tile([P, 4, 256], BF16, name="u_sb_%d" % i, tag="u")
+            nc.sync.dma_start(out=u_sb[i][:], in_=u_v[i])
+
+        def load_h(i):
+            h_sb[i] = hpool.tile([P, 2048], BF16, name="h_sb_%d" % i, tag="h")
+            nc.sync.dma_start(out=h_sb[i][:], in_=h_v[i])
+
+        def copy_on(eng, out_, in_):
+            if eng == "act":
+                nc.scalar.copy(out=out_, in_=in_)
+            else:
+                nc.vector.tensor_copy(out=out_, in_=in_)
+
+        def t_z(k):
+            ps = bank([P, 1024], BF16, "z_ps%d" % k)
+            for q in range(8):
+                nc.tensor.transpose(ps[:, q * P : (q + 1) * P], z_sb[k][:, q // 2, (q % 2) * P : (q % 2 + 1) * P], ident_b[:])
+            return ps
+
+        def x_z(k, ps, eng):
+            copy_on(eng, zT[k][:], ps[:])
+
+        def t_u(i):
+            ps = bank([P, 1024], BF16, "u_ps%d" % i)
+            for q in range(8):
+                nc.tensor.transpose(ps[:, q * P : (q + 1) * P], u_sb[i][:, q // 2, (q % 2) * P : (q % 2 + 1) * P], ident_b[:])
+            u_ps[i] = ps
+
+        def x_u(i, eng):
+            uT[i] = work.tile([P, 1024], BF16, name="uT_%d" % i, tag="uT")
+            copy_on(eng, uT[i][:], u_ps[i][:])
+
+        def words_T(src_f32, base, name):
+            ps = bank([P, 512], F32, name)
+            for q in range(4):
+                nc.tensor.transpose(ps[:, q * P : (q + 1) * P], src_f32[:, base + q * P : base + (q + 1) * P], ident_f[:])
+            return ps
+
+        def t_h(i, t):
+            h_ps[i, t] = words_T(h_sb[i][:].bitcast(F32), t * 512, "h_ps%d_%d" % (i, t))
+
+        def x_h(i, t, eng):
+            if t == 0:
+                hq[i] = work.tile([P, 2048], BF16, name="hq_%d" % i, tag="hq", align_bytes=64)
+            dst = hq[i][:].bitcast(F32)[:, t * 512 : (t + 1) * 512].rearrange("q (g f e) -> q g f e", g=2, e=2)
+            copy_on(eng, dst, h_ps[i, t][:].rearrange("q (g e f) -> q g f e", g=2, e=2))
+
+        def q_h(i):
+            ch[i] = work.tile([P, 512], U32, name="ch_%d" % i, tag="ch", align_bytes=64)
+            sh[i] = work.tile([P, 512], U8, name="sh_%d" % i, tag="sh", align_bytes=64)
+            nc.vector.quantize_mx(out=ch[i][:].bitcast(FP8X4), scales=sh[i][:], in_=hq[i][:])
+
+        def t_w(c, j):
+            return words_T(w_sb[c][:].bitcast(F32), j * 512, "w_ps%d_%d" % (c, j))
+
+        def x_w(c, j, ps, eng):
+            off = (c % 2) * 256 + j * P
+            dst = gW[c // 2][:].bitcast(F32).rearrange("q (g o e) -> q g o e", g=2, e=2)[:, :, off : off + P, :]
+            copy_on(eng, dst, ps[:].rearrange("q (g e o) -> q g o e", g=2, e=2))
+
+        def q_w(n):
+            nc.vector.quantize_mx(out=cW[n][:].bitcast(FP8X4), scales=sW[n][:], in_=gW[n][:])
+
+        def bias_mm(a, n):
+            ps = bank([P, 512], F32, "b_ps%d_%d" % (a, n))
+            nc.tensor.matmul(out=ps[:], lhsT=ones[:], rhs=bias_in[:, a, n * 512 : (n + 1) * 512], start=True, stop=True)
+            return ps
+
+        def bias_x(a, n, ps, eng):
+            dst = bias_sb[a][:, n * 512 : (n + 1) * 512].rearrange("q (c j p) -> q c j p", c=2, j=2)
+            copy_on(eng, dst, ps[:].rearrange("q (c p j) -> q c j p", c=2, j=2))
+
+        def lo(i, t, n):
+            ps = bank([P, 512], F32, "lo_ps%d_%d_%d" % (i, t, n))
+            q = (i % 4) * 2 + t
+            nc.tensor.matmul(out=ps[:], lhsT=zT[i // 4][:, q * P : (q + 1) * P], rhs=uT[i][:, n * 512 : (n + 1) * 512],
+                             start=True, stop=True)
+            lo_ps[i, t, n] = ps
+
+        def p1(i, t, n, eng):
+            if (i not in pre):
+                pre[i] = prep.tile([P, 2048], F32, name="pre_%d" % i, tag="pre")
+            dst = pre[i][:, t * 1024 + n * 512 : t * 1024 + (n + 1) * 512]
+            bia = bias_sb[i // 8][:, n * 512 : (n + 1) * 512]
+            if eng == "act":
+                nc.scalar.activation(out=dst, in_=lo_ps[i, t, n][:], func=ACTF.Copy, scale=1.0 / 128.0)
+                nc.gpsimd.tensor_tensor(out=dst, in0=dst, in1=bia, op=ALU.add)
+            else:
+                nc.vector.scalar_tensor_tensor(out=dst, in0=lo_ps[i, t, n][:], scalar=1.0 / 128.0, in1=bia,
+                                               op0=ALU.mult, op1=ALU.add)
+
+        def mx(i, t, n):
+            ps = bank([P, 512], F32, "mx_ps%d_%d_%d" % (i, t, n))
+            for g in range(2):
+                q = 2 * t + g
+                nc.tensor.matmul_mx(out=ps[:], lhsT=ch[i][:, q * P : (q + 1) * P].bitcast(FP8X4),
+                                    lhsT_scale=sh[i][:, q * P : (q + 1) * P],
+                                    rhs=cW[n][:, g * 512 : (g + 1) * 512].bitcast(FP8X4),
+                                    rhs_scale=sW[n][:, g * 512 : (g + 1) * 512], start=(g == 0), stop=(g == 1))
+            mx_ps[i, t, n] = ps
+
+        def p2(i, t, n):
+            dst = pre[i][:, t * 1024 + n * 512 : t * 1024 + (n + 1) * 512]
+            nc.vector.tensor_tensor(out=dst, in0=mx_ps[i, t, n][:], in1=dst, op=ALU.add)
+
+        def ge(i, t):
+            st = stg.tile([P, 1024], F32, name="st_%d_%d" % (i, t), tag="st")
+            nc.scalar.activation(out=st[:].rearrange("q (c p j) -> q c p j", c=4, j=2),
+                                 in_=pre[i][:, t * 1024 : (t + 1) * 1024].rearrange("q (c j p) -> q c p j", c=4, j=2),
+                                 func=ACTF.Gelu)
+            nc.sync.dma_start(out=o_v[i][:, t, :], in_=st[:])
+
+        load_z(0); load_u(0); load_h(0)
+        for c in range(4):
+            load_w(c)
+        for i in range(1, LOOKAHEAD_LOADS):
+            load_u(i); load_h(i)
+            if i == 3:
+                load_z(1)
+
+        ps = t_z(0); x_z(0, ps, "act")
+        t_u(0); x_u(0, "act")
+        pb = [bias_mm(0, n) for n in range(2)]
+        for n in range(2):
+            bias_x(0, n, pb[n], "dve")
+        t_h(0, 0); t_h(0, 1)
+        x_h(0, 0, "act"); x_h(0, 1, "dve")
+        for j in range(4):
+            lo(0, j // 2, j % 2)
+        for j in range(4):
+            p1(0, j // 2, j % 2, "dve" if j % 2 == 0 else "act")
+        q_h(0)
+        for c in range(4):
+            pw = [t_w(c, j) for j in range(2)]
+            x_w(c, 0, pw[0], "act"); x_w(c, 1, pw[1], "dve")
+            if c % 2 == 1:
+                q_w(c // 2)
+        t_h(1, 0); t_h(1, 1); t_u(1)
+        x_h(1, 0, "act"); x_h(1, 1, "act"); x_u(1, "act")
+        q_h(1)
+
+        late_ge = None
+        for s in range(UNITS):
+            nx = s + 2
+            if nx < UNITS:
+                zk = None
+                if nx % 4 == 0:
+                    zk = t_z(nx // 4)
+                    x_z(nx // 4, zk, "act")
+                t_h(nx, 0); t_h(nx, 1); t_u(nx)
+                x_h(nx, 0, "act"); x_h(nx, 1, "act"); x_u(nx, "act")
+            if s == 4:
+                pb = [bias_mm(1, n) for n in range(2)]
+                for n in range(2):
+                    bias_x(1, n, pb[n], "dve")
+            if late_ge is not None:
+                ge(*late_ge)
+            ld = s + LOOKAHEAD_LOADS
+            if ld < UNITS:
+                load_u(ld); load_h(ld)
+                if ld in (7, 11):
+                    load_z((ld + 1) // 4)
+            for j in range(4):
+                t, n = j // 2, j % 2
+                if s + 1 < UNITS:
+                    lo(s + 1, t, n)
+                mx(s, t, n)
+                if s + 1 < UNITS:
+                    p1(s + 1, t, n, "act" if j in ACT_P1 else "dve")
+                p2(s, t, n)
+                if j == 1:
+                    ge(s, 0)
+            if nx < UNITS:
+                q_h(nx)
+            late_ge = (s, 1)
+        ge(*late_ge)

@@ -15,9 +15,22 @@ FLOPS = 2 * 4096 * 1024 * 1024 + 2 * 4096 * 1024 * 128
 
 P = 128
 UNITS = 16
-LOOKAHEAD_LOADS = 6
-ACT_P1 = (3,)
+DU = 5
+DL = 4
+DH = 2
+PRE_BUFS = 6
+W_STEP = -2
+LOAD_AHEAD = 3
 MANUAL = True
+GROUP_LO = True
+
+
+def p1_engine(i, j):
+    if i < DL:
+        return "act" if j % 2 == 1 else "dve"
+    if j == 1 or (j == 2 and i % 4 == 0):
+        return "act"
+    return "dve"
 
 
 def tile_loratacmlp4_pb_t_kernel(tc, h, z, u, b, W_out, b_out, out):
@@ -35,7 +48,7 @@ def tile_loratacmlp4_pb_t_kernel(tc, h, z, u, b, W_out, b_out, out):
         hpool = ctx.enter_context(tc.tile_pool(name="hpool", bufs=8))
         upool = ctx.enter_context(tc.tile_pool(name="upool", bufs=8))
         work = ctx.enter_context(tc.tile_pool(name="work", bufs=3))
-        prep = ctx.enter_context(tc.tile_pool(name="prep", bufs=3))
+        prep = ctx.enter_context(tc.tile_pool(name="prep", bufs=PRE_BUFS))
         stg = ctx.enter_context(tc.tile_pool(name="stg", bufs=6))
         psum = ctx.enter_context(tc.psum_pool(name="psum", bufs=8))
         if MANUAL:
@@ -188,67 +201,87 @@ def tile_loratacmlp4_pb_t_kernel(tc, h, z, u, b, W_out, b_out, out):
                                  func=ACTF.Gelu)
             nc.sync.dma_start(out=o_v[i][:, t, :], in_=st[:])
 
-        load_z(0); load_u(0); load_h(0)
-        for c in range(4):
-            load_w(c)
-        for i in range(1, LOOKAHEAD_LOADS):
-            load_u(i); load_h(i)
-            if i == 3:
-                load_z(1)
+        def ge_half(i, t, n):
+            st = stg.tile([P, 512], F32, name="sth_%d_%d_%d" % (i, t, n), tag="st")
+            lo_c = t * 1024 + n * 512
+            nc.scalar.activation(out=st[:].rearrange("q (c p j) -> q c p j", c=2, j=2),
+                                 in_=pre[i][:, lo_c : lo_c + 512].rearrange("q (c j p) -> q c p j", c=2, j=2),
+                                 func=ACTF.Gelu)
+            nc.sync.dma_start(out=o_v[i][:, t, n * 512 : (n + 1) * 512], in_=st[:])
 
-        ps = t_z(0); x_z(0, ps, "act")
-        t_u(0); x_u(0, "act")
-        pb = [bias_mm(0, n) for n in range(2)]
-        for n in range(2):
-            bias_x(0, n, pb[n], "dve")
-        t_h(0, 0); t_h(0, 1)
-        x_h(0, 0, "act"); x_h(0, 1, "dve")
-        for j in range(4):
-            lo(0, j // 2, j % 2)
-        for j in range(4):
-            p1(0, j // 2, j % 2, "dve" if j % 2 == 0 else "act")
-        q_h(0)
+        loads = []
+        for i in range(UNITS):
+            loads.append((i - DU, 1, load_u, i))
+            loads.append((i - DH, 2, load_h, i))
+        for kk in range(4):
+            loads.append((4 * kk - DU, 0, load_z, kk))
         for c in range(4):
-            pw = [t_w(c, j) for j in range(2)]
-            x_w(c, 0, pw[0], "act"); x_w(c, 1, pw[1], "dve")
-            if c % 2 == 1:
-                q_w(c // 2)
-        t_h(1, 0); t_h(1, 1); t_u(1)
-        x_h(1, 0, "act"); x_h(1, 1, "act"); x_u(1, "act")
-        q_h(1)
+            loads.append((W_STEP - 0.5, c, load_w, c))
+        loads = sorted(loads, key=lambda e: (e[0], e[1]))
+        issued = [0]
 
+        def issue_loads(upto):
+            while issued[0] < len(loads) and loads[issued[0]][0] <= upto:
+                e = loads[issued[0]]
+                e[2](e[3])
+                issued[0] += 1
+
+        def w_prep():
+            for c in range(4):
+                pw = [t_w(c, j) for j in range(2)]
+                x_w(c, 0, pw[0], "act")
+                x_w(c, 1, pw[1], "dve")
+                if c % 2 == 1:
+                    q_w(c // 2)
+
+        issue_loads(-DU + LOAD_AHEAD)
         late_ge = None
-        for s in range(UNITS):
-            nx = s + 2
-            if nx < UNITS:
-                zk = None
-                if nx % 4 == 0:
-                    zk = t_z(nx // 4)
-                    x_z(nx // 4, zk, "act")
-                t_h(nx, 0); t_h(nx, 1); t_u(nx)
-                x_h(nx, 0, "act"); x_h(nx, 1, "act"); x_u(nx, "act")
-            if s == 4:
-                pb = [bias_mm(1, n) for n in range(2)]
+        for s in range(-DU, UNITS):
+            iu, il, ih = s + DU, s + DL, s + DH
+            if s == W_STEP:
+                w_prep()
+            zk = None
+            if iu % 4 == 0 and iu < UNITS:
+                zk = t_z(iu // 4)
+                x_z(iu // 4, zk, "act")
+            if 0 <= ih < UNITS:
+                t_h(ih, 0)
+                t_h(ih, 1)
+            if iu < UNITS:
+                t_u(iu)
+            if 0 <= ih < UNITS:
+                x_h(ih, 0, "act")
+                x_h(ih, 1, "act")
+            if iu < UNITS:
+                x_u(iu, "act")
+            if il in (0, 8):
+                pb = [bias_mm(il // 8, n) for n in range(2)]
                 for n in range(2):
-                    bias_x(1, n, pb[n], "dve")
+                    bias_x(il // 8, n, pb[n], "dve")
             if late_ge is not None:
                 ge(*late_ge)
-            ld = s + LOOKAHEAD_LOADS
-            if ld < UNITS:
-                load_u(ld); load_h(ld)
-                if ld in (7, 11):
-                    load_z((ld + 1) // 4)
+                late_ge = None
+            issue_loads(s + 1 + LOAD_AHEAD)
+            if GROUP_LO and 0 <= il < UNITS:
+                for j in range(4):
+                    lo(il, j // 2, j % 2)
+                for j in range(4):
+                    p1(il, j // 2, j % 2, p1_engine(il, j))
             for j in range(4):
                 t, n = j // 2, j % 2
-                if s + 1 < UNITS:
-                    lo(s + 1, t, n)
-                mx(s, t, n)
-                if s + 1 < UNITS:
-                    p1(s + 1, t, n, "act" if j in ACT_P1 else "dve")
-                p2(s, t, n)
-                if j == 1:
-                    ge(s, 0)
-            if nx < UNITS:
-                q_h(nx)
-            late_ge = (s, 1)
-        ge(*late_ge)
+                if 0 <= il < UNITS and not GROUP_LO:
+                    lo(il, t, n)
+                if s >= 0:
+                    mx(s, t, n)
+                if 0 <= il < UNITS and not GROUP_LO:
+                    p1(il, t, n, p1_engine(il, j))
+                if s >= 0:
+                    p2(s, t, n)
+                    if s == UNITS - 1:
+                        ge_half(s, t, n)
+                    elif j == 1:
+                        ge(s, 0)
+            if 0 <= ih < UNITS:
+                q_h(ih)
+            if 0 <= s < UNITS - 1:
+                late_ge = (s, 1)

@@ -23,6 +23,7 @@ W_STEP = -2
 LOAD_AHEAD = 3
 MANUAL = True
 GROUP_LO = True
+STORE_Q = "sp"
 
 
 def p1_engine(i, j):
@@ -37,8 +38,8 @@ def tile_loratacmlp4_pb_t_kernel(tc, h, z, u, b, W_out, b_out, out):
     nc = tc.nc
     h_v = h.rearrange("a k (p t) c -> (a k) p (t c)", t=2)
     z_v = z.rearrange("a k (p t) r -> p (a k) (t r)", t=2)
-    u_v = u.rearrange("a k (c p j) r -> (a k) p c (j r)", c=4, j=2)
-    w_v = W_out.rearrange("(c p j) k -> c p (j k)", c=4, j=2)
+    u_v = u.rearrange("a k (n p j) r -> (a k) p n (j r)", n=2, j=4)
+    w_v = W_out.rearrange("(c j p) k -> c p j k", c=4, j=2)
     o_v = out.rearrange("a k (p t) o -> (a k) p t o", t=2)
     b_v = b.rearrange("a x y o -> (x y) a o")
     bo_v = b_out.rearrange("(x o) -> x o", x=1)
@@ -49,7 +50,7 @@ def tile_loratacmlp4_pb_t_kernel(tc, h, z, u, b, W_out, b_out, out):
         upool = ctx.enter_context(tc.tile_pool(name="upool", bufs=8))
         work = ctx.enter_context(tc.tile_pool(name="work", bufs=3))
         prep = ctx.enter_context(tc.tile_pool(name="prep", bufs=PRE_BUFS))
-        stg = ctx.enter_context(tc.tile_pool(name="stg", bufs=6))
+        stg = ctx.enter_context(tc.tile_pool(name="stg", bufs=3))
         psum = ctx.enter_context(tc.psum_pool(name="psum", bufs=8))
         if MANUAL:
             ctx.enter_context(tc.manual_schedule())
@@ -74,7 +75,7 @@ def tile_loratacmlp4_pb_t_kernel(tc, h, z, u, b, W_out, b_out, out):
 
         z_sb = [const.tile([P, 4, 256], BF16, name="z_sb%d" % k) for k in range(4)]
         zT = [const.tile([P, 1024], BF16, name="zT%d" % k) for k in range(4)]
-        w_sb = [const.tile([P, 2048], BF16, name="w_sb%d" % c) for c in range(4)]
+        w_sb = [const.tile([P, 2, 1024], BF16, name="w_sb%d" % c) for c in range(4)]
         gW = [const.tile([P, 4096], BF16, name="gW%d" % n, align_bytes=64) for n in range(2)]
         cW = [const.tile([P, 1024], U32, name="cW%d" % n, align_bytes=64) for n in range(2)]
         sW = [const.tile([P, 1024], U8, name="sW%d" % n, align_bytes=64) for n in range(2)]
@@ -89,7 +90,7 @@ def tile_loratacmlp4_pb_t_kernel(tc, h, z, u, b, W_out, b_out, out):
             nc.sync.dma_start(out=w_sb[c][:], in_=w_v[c])
 
         def load_u(i):
-            u_sb[i] = upool.tile([P, 4, 256], BF16, name="u_sb_%d" % i, tag="u")
+            u_sb[i] = upool.tile([P, 2, 512], BF16, name="u_sb_%d" % i, tag="u")
             nc.sync.dma_start(out=u_sb[i][:], in_=u_v[i])
 
         def load_h(i):
@@ -114,7 +115,7 @@ def tile_loratacmlp4_pb_t_kernel(tc, h, z, u, b, W_out, b_out, out):
         def t_u(i):
             ps = bank([P, 1024], BF16, "u_ps%d" % i)
             for q in range(8):
-                nc.tensor.transpose(ps[:, q * P : (q + 1) * P], u_sb[i][:, q // 2, (q % 2) * P : (q % 2 + 1) * P], ident_b[:])
+                nc.tensor.transpose(ps[:, q * P : (q + 1) * P], u_sb[i][:, q // 4, (q % 4) * P : (q % 4 + 1) * P], ident_b[:])
             u_ps[i] = ps
 
         def x_u(i, eng):
@@ -142,7 +143,7 @@ def tile_loratacmlp4_pb_t_kernel(tc, h, z, u, b, W_out, b_out, out):
             nc.vector.quantize_mx(out=ch[i][:].bitcast(FP8X4), scales=sh[i][:], in_=hq[i][:])
 
         def t_w(c, j):
-            return words_T(w_sb[c][:].bitcast(F32), j * 512, "w_ps%d_%d" % (c, j))
+            return words_T(w_sb[c][:, j, :].bitcast(F32), 0, "w_ps%d_%d" % (c, j))
 
         def x_w(c, j, ps, eng):
             off = (c % 2) * 256 + j * P
@@ -158,8 +159,7 @@ def tile_loratacmlp4_pb_t_kernel(tc, h, z, u, b, W_out, b_out, out):
             return ps
 
         def bias_x(a, n, ps, eng):
-            dst = bias_sb[a][:, n * 512 : (n + 1) * 512].rearrange("q (c j p) -> q c j p", c=2, j=2)
-            copy_on(eng, dst, ps[:].rearrange("q (c p j) -> q c j p", c=2, j=2))
+            copy_on(eng, bias_sb[a][:, n * 512 : (n + 1) * 512], ps[:])
 
         def lo(i, t, n):
             ps = bank([P, 512], F32, "lo_ps%d_%d_%d" % (i, t, n))
@@ -173,12 +173,14 @@ def tile_loratacmlp4_pb_t_kernel(tc, h, z, u, b, W_out, b_out, out):
                 pre[i] = prep.tile([P, 2048], F32, name="pre_%d" % i, tag="pre")
             dst = pre[i][:, t * 1024 + n * 512 : t * 1024 + (n + 1) * 512]
             bia = bias_sb[i // 8][:, n * 512 : (n + 1) * 512]
+            dst_pj = dst.rearrange("q (p j) -> q p j", j=4)
+            src_pj = lo_ps[i, t, n][:].rearrange("q (j p) -> q p j", j=4)
             if eng == "act":
-                nc.scalar.activation(out=dst, in_=lo_ps[i, t, n][:], func=ACTF.Copy, scale=1.0 / 128.0)
+                nc.scalar.activation(out=dst_pj, in_=src_pj, func=ACTF.Copy, scale=1.0 / 128.0)
                 nc.gpsimd.tensor_tensor(out=dst, in0=dst, in1=bia, op=ALU.add)
             else:
-                nc.vector.scalar_tensor_tensor(out=dst, in0=lo_ps[i, t, n][:], scalar=1.0 / 128.0, in1=bia,
-                                               op0=ALU.mult, op1=ALU.add)
+                nc.vector.scalar_tensor_tensor(out=dst_pj, in0=src_pj, scalar=1.0 / 128.0,
+                                               in1=bia.rearrange("q (p j) -> q p j", j=4), op0=ALU.mult, op1=ALU.add)
 
         def mx(i, t, n):
             ps = bank([P, 512], F32, "mx_ps%d_%d_%d" % (i, t, n))
@@ -194,19 +196,25 @@ def tile_loratacmlp4_pb_t_kernel(tc, h, z, u, b, W_out, b_out, out):
             dst = pre[i][:, t * 1024 + n * 512 : t * 1024 + (n + 1) * 512]
             nc.vector.tensor_tensor(out=dst, in0=mx_ps[i, t, n][:], in1=dst, op=ALU.add)
 
+        def store(out_, in_):
+            if STORE_Q == "pool":
+                nc.gpsimd.dma_start(out=out_, in_=in_)
+            else:
+                nc.sync.dma_start(out=out_, in_=in_)
+
+        stage = {}
+
         def ge(i, t):
-            st = stg.tile([P, 1024], F32, name="st_%d_%d" % (i, t), tag="st")
-            nc.scalar.activation(out=st[:].rearrange("q (c p j) -> q c p j", c=4, j=2),
-                                 in_=pre[i][:, t * 1024 : (t + 1) * 1024].rearrange("q (c j p) -> q c p j", c=4, j=2),
-                                 func=ACTF.Gelu)
-            nc.sync.dma_start(out=o_v[i][:, t, :], in_=st[:])
+            if t == 0:
+                stage[i] = stg.tile([P, 2, 1024], F32, name="st_%d" % i, tag="st")
+            nc.scalar.activation(out=stage[i][:, t, :], in_=pre[i][:, t * 1024 : (t + 1) * 1024], func=ACTF.Gelu)
+            if t == 1:
+                store(o_v[i], stage[i][:])
 
         def ge_half(i, t, n):
-            st = stg.tile([P, 512], F32, name="sth_%d_%d_%d" % (i, t, n), tag="st")
+            st = stg.tile([P, 512], F32, name="sth_%d_%d_%d" % (i, t, n), tag="sth", bufs=4)
             lo_c = t * 1024 + n * 512
-            nc.scalar.activation(out=st[:].rearrange("q (c p j) -> q c p j", c=2, j=2),
-                                 in_=pre[i][:, lo_c : lo_c + 512].rearrange("q (c j p) -> q c p j", c=2, j=2),
-                                 func=ACTF.Gelu)
+            nc.scalar.activation(out=st[:], in_=pre[i][:, lo_c : lo_c + 512], func=ACTF.Gelu)
             nc.sync.dma_start(out=o_v[i][:, t, n * 512 : (n + 1) * 512], in_=st[:])
 
         loads = []

@@ -15,7 +15,7 @@ FLOPS = 2 * 4096 * 1024 * 1024 + 2 * 4096 * 1024 * 128
 
 P = 128
 UNITS = 16
-DU = 5
+DU = 6
 DL = 4
 DH = 2
 PRE_BUFS = 6
@@ -23,7 +23,6 @@ W_STEP = -2
 LOAD_AHEAD = 3
 MANUAL = True
 GROUP_LO = True
-STORE_Q = "sp"
 
 
 def p1_engine(i, j):
@@ -38,8 +37,8 @@ def tile_loratacmlp4_pb_t_kernel(tc, h, z, u, b, W_out, b_out, out):
     nc = tc.nc
     h_v = h.rearrange("a k (p t) c -> (a k) p (t c)", t=2)
     z_v = z.rearrange("a k (p t) r -> p (a k) (t r)", t=2)
-    u_v = u.rearrange("a k (n p j) r -> (a k) p n (j r)", n=2, j=4)
-    w_v = W_out.rearrange("(c j p) k -> c p j k", c=4, j=2)
+    u_v = u.rearrange("a k (c p j) r -> (a k) p c (j r)", c=4, j=2)
+    w_v = W_out.rearrange("(c p j) k -> c p (j k)", c=4, j=2)
     o_v = out.rearrange("a k (p t) o -> (a k) p t o", t=2)
     b_v = b.rearrange("a x y o -> (x y) a o")
     bo_v = b_out.rearrange("(x o) -> x o", x=1)
@@ -50,7 +49,7 @@ def tile_loratacmlp4_pb_t_kernel(tc, h, z, u, b, W_out, b_out, out):
         upool = ctx.enter_context(tc.tile_pool(name="upool", bufs=8))
         work = ctx.enter_context(tc.tile_pool(name="work", bufs=3))
         prep = ctx.enter_context(tc.tile_pool(name="prep", bufs=PRE_BUFS))
-        stg = ctx.enter_context(tc.tile_pool(name="stg", bufs=3))
+        stg = ctx.enter_context(tc.tile_pool(name="stg", bufs=6))
         psum = ctx.enter_context(tc.psum_pool(name="psum", bufs=8))
         if MANUAL:
             ctx.enter_context(tc.manual_schedule())
@@ -75,7 +74,7 @@ def tile_loratacmlp4_pb_t_kernel(tc, h, z, u, b, W_out, b_out, out):
 
         z_sb = [const.tile([P, 4, 256], BF16, name="z_sb%d" % k) for k in range(4)]
         zT = [const.tile([P, 1024], BF16, name="zT%d" % k) for k in range(4)]
-        w_sb = [const.tile([P, 2, 1024], BF16, name="w_sb%d" % c) for c in range(4)]
+        w_sb = [const.tile([P, 2048], BF16, name="w_sb%d" % c) for c in range(4)]
         gW = [const.tile([P, 4096], BF16, name="gW%d" % n, align_bytes=64) for n in range(2)]
         cW = [const.tile([P, 1024], U32, name="cW%d" % n, align_bytes=64) for n in range(2)]
         sW = [const.tile([P, 1024], U8, name="sW%d" % n, align_bytes=64) for n in range(2)]
@@ -90,7 +89,7 @@ def tile_loratacmlp4_pb_t_kernel(tc, h, z, u, b, W_out, b_out, out):
             nc.sync.dma_start(out=w_sb[c][:], in_=w_v[c])
 
         def load_u(i):
-            u_sb[i] = upool.tile([P, 2, 512], BF16, name="u_sb_%d" % i, tag="u")
+            u_sb[i] = upool.tile([P, 4, 256], BF16, name="u_sb_%d" % i, tag="u")
             nc.sync.dma_start(out=u_sb[i][:], in_=u_v[i])
 
         def load_h(i):
@@ -115,11 +114,11 @@ def tile_loratacmlp4_pb_t_kernel(tc, h, z, u, b, W_out, b_out, out):
         def t_u(i):
             ps = bank([P, 1024], BF16, "u_ps%d" % i)
             for q in range(8):
-                nc.tensor.transpose(ps[:, q * P : (q + 1) * P], u_sb[i][:, q // 4, (q % 4) * P : (q % 4 + 1) * P], ident_b[:])
+                nc.tensor.transpose(ps[:, q * P : (q + 1) * P], u_sb[i][:, q // 2, (q % 2) * P : (q % 2 + 1) * P], ident_b[:])
             u_ps[i] = ps
 
         def x_u(i, eng):
-            uT[i] = work.tile([P, 1024], BF16, name="uT_%d" % i, tag="uT")
+            uT[i] = work.tile([P, 1024], BF16, name="uT_%d" % i, tag="uT", bufs=4)
             copy_on(eng, uT[i][:], u_ps[i][:])
 
         def words_T(src_f32, base, name):
@@ -143,7 +142,7 @@ def tile_loratacmlp4_pb_t_kernel(tc, h, z, u, b, W_out, b_out, out):
             nc.vector.quantize_mx(out=ch[i][:].bitcast(FP8X4), scales=sh[i][:], in_=hq[i][:])
 
         def t_w(c, j):
-            return words_T(w_sb[c][:, j, :].bitcast(F32), 0, "w_ps%d_%d" % (c, j))
+            return words_T(w_sb[c][:].bitcast(F32), j * 512, "w_ps%d_%d" % (c, j))
 
         def x_w(c, j, ps, eng):
             off = (c % 2) * 256 + j * P
@@ -159,7 +158,8 @@ def tile_loratacmlp4_pb_t_kernel(tc, h, z, u, b, W_out, b_out, out):
             return ps
 
         def bias_x(a, n, ps, eng):
-            copy_on(eng, bias_sb[a][:, n * 512 : (n + 1) * 512], ps[:])
+            dst = bias_sb[a][:, n * 512 : (n + 1) * 512].rearrange("q (c j p) -> q c j p", c=2, j=2)
+            copy_on(eng, dst, ps[:].rearrange("q (c p j) -> q c j p", c=2, j=2))
 
         def lo(i, t, n):
             ps = bank([P, 512], F32, "lo_ps%d_%d_%d" % (i, t, n))
@@ -173,14 +173,12 @@ def tile_loratacmlp4_pb_t_kernel(tc, h, z, u, b, W_out, b_out, out):
                 pre[i] = prep.tile([P, 2048], F32, name="pre_%d" % i, tag="pre")
             dst = pre[i][:, t * 1024 + n * 512 : t * 1024 + (n + 1) * 512]
             bia = bias_sb[i // 8][:, n * 512 : (n + 1) * 512]
-            dst_pj = dst.rearrange("q (p j) -> q p j", j=4)
-            src_pj = lo_ps[i, t, n][:].rearrange("q (j p) -> q p j", j=4)
             if eng == "act":
-                nc.scalar.activation(out=dst_pj, in_=src_pj, func=ACTF.Copy, scale=1.0 / 128.0)
+                nc.scalar.activation(out=dst, in_=lo_ps[i, t, n][:], func=ACTF.Copy, scale=1.0 / 128.0)
                 nc.gpsimd.tensor_tensor(out=dst, in0=dst, in1=bia, op=ALU.add)
             else:
-                nc.vector.scalar_tensor_tensor(out=dst_pj, in0=src_pj, scalar=1.0 / 128.0,
-                                               in1=bia.rearrange("q (p j) -> q p j", j=4), op0=ALU.mult, op1=ALU.add)
+                nc.vector.scalar_tensor_tensor(out=dst, in0=lo_ps[i, t, n][:], scalar=1.0 / 128.0, in1=bia,
+                                               op0=ALU.mult, op1=ALU.add)
 
         def mx(i, t, n):
             ps = bank([P, 512], F32, "mx_ps%d_%d_%d" % (i, t, n))
@@ -196,25 +194,19 @@ def tile_loratacmlp4_pb_t_kernel(tc, h, z, u, b, W_out, b_out, out):
             dst = pre[i][:, t * 1024 + n * 512 : t * 1024 + (n + 1) * 512]
             nc.vector.tensor_tensor(out=dst, in0=mx_ps[i, t, n][:], in1=dst, op=ALU.add)
 
-        def store(out_, in_):
-            if STORE_Q == "pool":
-                nc.gpsimd.dma_start(out=out_, in_=in_)
-            else:
-                nc.sync.dma_start(out=out_, in_=in_)
-
-        stage = {}
-
         def ge(i, t):
-            if t == 0:
-                stage[i] = stg.tile([P, 2, 1024], F32, name="st_%d" % i, tag="st")
-            nc.scalar.activation(out=stage[i][:, t, :], in_=pre[i][:, t * 1024 : (t + 1) * 1024], func=ACTF.Gelu)
-            if t == 1:
-                store(o_v[i], stage[i][:])
+            st = stg.tile([P, 1024], F32, name="st_%d_%d" % (i, t), tag="st")
+            nc.scalar.activation(out=st[:].rearrange("q (c p j) -> q c p j", c=4, j=2),
+                                 in_=pre[i][:, t * 1024 : (t + 1) * 1024].rearrange("q (c j p) -> q c p j", c=4, j=2),
+                                 func=ACTF.Gelu)
+            nc.sync.dma_start(out=o_v[i][:, t, :], in_=st[:])
 
         def ge_half(i, t, n):
-            st = stg.tile([P, 512], F32, name="sth_%d_%d_%d" % (i, t, n), tag="sth", bufs=4)
+            st = stg.tile([P, 512], F32, name="sth_%d_%d_%d" % (i, t, n), tag="st")
             lo_c = t * 1024 + n * 512
-            nc.scalar.activation(out=st[:], in_=pre[i][:, lo_c : lo_c + 512], func=ACTF.Gelu)
+            nc.scalar.activation(out=st[:].rearrange("q (c p j) -> q c p j", c=2, j=2),
+                                 in_=pre[i][:, lo_c : lo_c + 512].rearrange("q (c j p) -> q c p j", c=2, j=2),
+                                 func=ACTF.Gelu)
             nc.sync.dma_start(out=o_v[i][:, t, n * 512 : (n + 1) * 512], in_=st[:])
 
         loads = []
@@ -248,6 +240,15 @@ def tile_loratacmlp4_pb_t_kernel(tc, h, z, u, b, W_out, b_out, out):
             iu, il, ih = s + DU, s + DL, s + DH
             if s == W_STEP:
                 w_prep()
+            if il in (0, 8):
+                pb = [bias_mm(il // 8, n) for n in range(2)]
+                for n in range(2):
+                    bias_x(il // 8, n, pb[n], "dve")
+            if 0 <= il < UNITS:
+                for j in range(2):
+                    lo(il, j // 2, j % 2)
+                for j in range(2):
+                    p1(il, j // 2, j % 2, p1_engine(il, j))
             zk = None
             if iu % 4 == 0 and iu < UNITS:
                 zk = t_z(iu // 4)
@@ -262,18 +263,14 @@ def tile_loratacmlp4_pb_t_kernel(tc, h, z, u, b, W_out, b_out, out):
                 x_h(ih, 1, "act")
             if iu < UNITS:
                 x_u(iu, "act")
-            if il in (0, 8):
-                pb = [bias_mm(il // 8, n) for n in range(2)]
-                for n in range(2):
-                    bias_x(il // 8, n, pb[n], "dve")
             if late_ge is not None:
                 ge(*late_ge)
                 late_ge = None
             issue_loads(s + 1 + LOAD_AHEAD)
             if GROUP_LO and 0 <= il < UNITS:
-                for j in range(4):
+                for j in range(2, 4):
                     lo(il, j // 2, j % 2)
-                for j in range(4):
+                for j in range(2, 4):
                     p1(il, j // 2, j % 2, p1_engine(il, j))
             for j in range(4):
                 t, n = j // 2, j % 2

@@ -19,18 +19,21 @@ DU = 6
 DL = 4
 DH = 2
 PRE_BUFS = 6
-W_STEP = -2
+W_STEP = -2.5
+W_AT = {-3: (0, 1), -2: (2, 3)}
 LOAD_AHEAD = 3
 MANUAL = True
+ACT_J = [(1, 2), (1,), (1,), (1,)]
+XU_ENG = "act"
+HEAD_ACT = (1, 3)
+XW_ACT = (0,)
 GROUP_LO = True
 
 
 def p1_engine(i, j):
     if i < DL:
-        return "act" if j % 2 == 1 else "dve"
-    if j == 1 or (j == 2 and i % 4 == 0):
-        return "act"
-    return "dve"
+        return "act" if j in HEAD_ACT else "dve"
+    return "act" if j in ACT_J[i % len(ACT_J)] else "dve"
 
 
 def tile_loratacmlp4_pb_t_kernel(tc, h, z, u, b, W_out, b_out, out):
@@ -226,61 +229,67 @@ def tile_loratacmlp4_pb_t_kernel(tc, h, z, u, b, W_out, b_out, out):
                 e[2](e[3])
                 issued[0] += 1
 
-        def w_prep():
-            for c in range(4):
-                pw = [t_w(c, j) for j in range(2)]
-                x_w(c, 0, pw[0], "act")
-                x_w(c, 1, pw[1], "dve")
-                if c % 2 == 1:
-                    q_w(c // 2)
-
         issue_loads(-DU + LOAD_AHEAD)
         late_ge = None
         for s in range(-DU, UNITS):
             iu, il, ih = s + DU, s + DL, s + DH
-            if s == W_STEP:
-                w_prep()
+            runs = []
+            for c in W_AT.get(s, ()):
+                for j in range(2):
+                    runs.append(("w", c, j))
+            if 0 <= ih < UNITS:
+                runs.append(("h", ih, 0))
+                runs.append(("h", ih, 1))
+            if iu % 4 == 0 and iu < UNITS:
+                runs.append(("z", iu // 4, 0))
+            if iu < UNITS:
+                runs.append(("u", iu, 0))
             if il in (0, 8):
                 pb = [bias_mm(il // 8, n) for n in range(2)]
                 for n in range(2):
                     bias_x(il // 8, n, pb[n], "dve")
-            if 0 <= il < UNITS:
-                for j in range(2):
+            has_lo = 0 <= il < UNITS
+            gaps = 3 if has_lo else 1
+            per_gap = (len(runs) + gaps - 1) // gaps
+            done = 0
+            for j in range(4):
+                if has_lo:
                     lo(il, j // 2, j % 2)
-                for j in range(2):
                     p1(il, j // 2, j % 2, p1_engine(il, j))
-            zk = None
-            if iu % 4 == 0 and iu < UNITS:
-                zk = t_z(iu // 4)
-                x_z(iu // 4, zk, "act")
-            if 0 <= ih < UNITS:
-                t_h(ih, 0)
-                t_h(ih, 1)
-            if iu < UNITS:
-                t_u(iu)
-            if 0 <= ih < UNITS:
-                x_h(ih, 0, "act")
-                x_h(ih, 1, "act")
-            if iu < UNITS:
-                x_u(iu, "act")
+                if j < gaps:
+                    todo = runs[done : done + per_gap]
+                    done += len(todo)
+                    held = []
+                    for kind, a, bb in todo:
+                        if kind == "w":
+                            held.append(t_w(a, bb))
+                        elif kind == "h":
+                            t_h(a, bb)
+                            held.append(None)
+                        elif kind == "z":
+                            held.append(t_z(a))
+                        else:
+                            t_u(a)
+                            held.append(None)
+                    for (kind, a, bb), ps in zip(todo, held):
+                        if kind == "w":
+                            x_w(a, bb, ps, "act" if bb in XW_ACT else "dve")
+                            if bb == 1 and a % 2 == 1:
+                                q_w(a // 2)
+                        elif kind == "h":
+                            x_h(a, bb, "act")
+                        elif kind == "z":
+                            x_z(a, ps, XU_ENG)
+                        else:
+                            x_u(a, XU_ENG)
             if late_ge is not None:
                 ge(*late_ge)
                 late_ge = None
             issue_loads(s + 1 + LOAD_AHEAD)
-            if GROUP_LO and 0 <= il < UNITS:
-                for j in range(2, 4):
-                    lo(il, j // 2, j % 2)
-                for j in range(2, 4):
-                    p1(il, j // 2, j % 2, p1_engine(il, j))
             for j in range(4):
                 t, n = j // 2, j % 2
-                if 0 <= il < UNITS and not GROUP_LO:
-                    lo(il, t, n)
                 if s >= 0:
                     mx(s, t, n)
-                if 0 <= il < UNITS and not GROUP_LO:
-                    p1(il, t, n, p1_engine(il, j))
-                if s >= 0:
                     p2(s, t, n)
                     if s == UNITS - 1:
                         ge_half(s, t, n)

@@ -68,12 +68,18 @@ def tile_loratacmlp4_pb_t_kernel(tc, h, z, u, b, W_out, b_out, out):
         nc.vector.memset(ones[:], 1.0)
         bias_in = const.tile([P, 2, 1024], BF16, name="bias_in")
         nc.vector.memset(bias_in[:], 0.0)
+        c128 = const.tile([P, P], BF16, name="c128")
+        nc.vector.memset(c128[:], 128.0)
+        bias_pm = const.tile([P, 2048], BF16, name="bias_pm")
         warm = const.tile([P, 1], F32, name="warm")
         nc.vector.memset(warm[:], 0.0)
         nc.scalar.activation(out=warm[:], in_=warm[:], func=ACTF.Gelu)
         nc.scalar.dma_start(out=bias_in[1:2, :, :], in_=b_v)
         for a in range(2):
             nc.scalar.dma_start(out=bias_in[0:1, a, :], in_=bo_v)
+
+        nc.vector.tensor_copy(out=bias_pm[:].rearrange("q (m j p) -> q m j p", m=8, j=2),
+                              in_=bias_in[:].rearrange("q a (c p j) -> q (a c) j p", c=4, j=2))
 
         z_sb = [const.tile([P, 4, 256], BF16, name="z_sb%d" % k) for k in range(4)]
         zT = [const.tile([P, 1024], BF16, name="zT%d" % k) for k in range(4)]
@@ -114,11 +120,12 @@ def tile_loratacmlp4_pb_t_kernel(tc, h, z, u, b, W_out, b_out, out):
         def x_z(k, ps, eng):
             copy_on(eng, zT[k][:], ps[:])
 
-        def t_u(i):
-            ps = bank([P, 1024], BF16, "u_ps%d" % i)
-            for q in range(8):
+        def t_u(i, half):
+            if half == 0:
+                u_ps[i] = bank([P, 1024], BF16, "u_ps%d" % i)
+            ps = u_ps[i]
+            for q in range(4 * half, 4 * half + 4):
                 nc.tensor.transpose(ps[:, q * P : (q + 1) * P], u_sb[i][:, q // 2, (q % 2) * P : (q % 2 + 1) * P], ident_b[:])
-            u_ps[i] = ps
 
         def x_u(i, eng):
             uT[i] = work.tile([P, 1024], BF16, name="uT_%d" % i, tag="uT", bufs=4)
@@ -168,8 +175,13 @@ def tile_loratacmlp4_pb_t_kernel(tc, h, z, u, b, W_out, b_out, out):
             ps = bank([P, 512], F32, "lo_ps%d_%d_%d" % (i, t, n))
             q = (i % 4) * 2 + t
             nc.tensor.matmul(out=ps[:], lhsT=zT[i // 4][:, q * P : (q + 1) * P], rhs=uT[i][:, n * 512 : (n + 1) * 512],
-                             start=True, stop=True)
+                             start=True, stop=p1_engine(i, 2 * t + n) != "act")
             lo_ps[i, t, n] = ps
+
+        def lo_bias(i, t, n):
+            m = (i // 8) * 2 + n
+            nc.tensor.matmul(out=lo_ps[i, t, n][:], lhsT=c128[:], rhs=bias_pm[:, m * 512 : (m + 1) * 512],
+                             start=False, stop=True)
 
         def p1(i, t, n, eng):
             if (i not in pre):
@@ -178,7 +190,6 @@ def tile_loratacmlp4_pb_t_kernel(tc, h, z, u, b, W_out, b_out, out):
             bia = bias_sb[i // 8][:, n * 512 : (n + 1) * 512]
             if eng == "act":
                 nc.scalar.activation(out=dst, in_=lo_ps[i, t, n][:], func=ACTF.Copy, scale=1.0 / 128.0)
-                nc.gpsimd.tensor_tensor(out=dst, in0=dst, in1=bia, op=ALU.add)
             else:
                 nc.vector.scalar_tensor_tensor(out=dst, in0=lo_ps[i, t, n][:], scalar=1.0 / 128.0, in1=bia,
                                                op0=ALU.mult, op1=ALU.add)
@@ -244,19 +255,30 @@ def tile_loratacmlp4_pb_t_kernel(tc, h, z, u, b, W_out, b_out, out):
                 runs.append(("z", iu // 4, 0))
             if iu < UNITS:
                 runs.append(("u", iu, 0))
+                runs.append(("u", iu, 1))
             if il in (0, 8):
                 pb = [bias_mm(il // 8, n) for n in range(2)]
                 for n in range(2):
                     bias_x(il // 8, n, pb[n], "dve")
-            has_lo = 0 <= il < UNITS
-            gaps = 3 if has_lo else 1
+            slots = []
+            if 0 <= il < UNITS:
+                for j in range(4):
+                    slots.append(("lo", j))
+                    if p1_engine(il, j) == "act":
+                        slots.append(("bias", j))
+            gaps = max(len(slots) - 1, 1)
             per_gap = (len(runs) + gaps - 1) // gaps
             done = 0
-            for j in range(4):
-                if has_lo:
-                    lo(il, j // 2, j % 2)
-                    p1(il, j // 2, j % 2, p1_engine(il, j))
-                if j < gaps:
+            for k in range(max(len(slots), 1)):
+                if slots:
+                    kind, j = slots[k]
+                    if kind == "lo":
+                        lo(il, j // 2, j % 2)
+                    else:
+                        lo_bias(il, j // 2, j % 2)
+                    if kind == "bias" or p1_engine(il, j) != "act":
+                        p1(il, j // 2, j % 2, p1_engine(il, j))
+                if k < gaps:
                     todo = runs[done : done + per_gap]
                     done += len(todo)
                     held = []
@@ -269,7 +291,7 @@ def tile_loratacmlp4_pb_t_kernel(tc, h, z, u, b, W_out, b_out, out):
                         elif kind == "z":
                             held.append(t_z(a))
                         else:
-                            t_u(a)
+                            t_u(a, bb)
                             held.append(None)
                     for (kind, a, bb), ps in zip(todo, held):
                         if kind == "w":
@@ -280,7 +302,7 @@ def tile_loratacmlp4_pb_t_kernel(tc, h, z, u, b, W_out, b_out, out):
                             x_h(a, bb, "act")
                         elif kind == "z":
                             x_z(a, ps, XU_ENG)
-                        else:
+                        elif bb == 1:
                             x_u(a, XU_ENG)
             if late_ge is not None:
                 ge(*late_ge)

@@ -23,7 +23,7 @@ W_STEP = -2.5
 W_AT = {-3: (0, 1), -2: (2, 3)}
 LOAD_AHEAD = 3
 MANUAL = True
-ACT_J = [(1, 2), (1,), (1,), (1,)]
+ACT_J = [(1, 2), (1, 3), (1, 2), (1,)]
 XU_ENG = "act"
 HEAD_ACT = (1, 3)
 XW_ACT = (0,)

from contextlib import ExitStack

import concourse.mybir as mybir
from concourse.masks import make_identity

F32 = mybir.dt.float32
BF16 = mybir.dt.bfloat16
U32 = mybir.dt.uint32
U8 = mybir.dt.uint8
FP8X4 = mybir.dt.float8_e4m3fn_x4
ACTF = mybir.ActivationFunctionType
ALU = mybir.AluOpType

FLOPS = 2 * 4096 * 1024 * 1024 + 2 * 4096 * 1024 * 128

P = 128
UNITS = 16
DU = 6
DL = 4
DH = 2
PRE_BUFS = 6
W_STEP = -2.5
W_AT = {-3: (0, 1), -2: (2, 3)}
LOAD_AHEAD = 3
MANUAL = True
ACT_J = [(1, 2), (1, 3), (1, 2), (1,)]
XU_ENG = "act"
HEAD_ACT = (1, 3)
XW_ACT = (0,)
GROUP_LO = True


def p1_engine(i, j):
    if i < DL:
        return "act" if j in HEAD_ACT else "dve"
    return "act" if j in ACT_J[i % len(ACT_J)] else "dve"


def tile_loratacmlp4_pb_t_kernel(tc, h, z, u, b, W_out, b_out, out):
    nc = tc.nc
    h_v = h.rearrange("a k (p t) c -> (a k) p (t c)", t=2)
    z_v = z.rearrange("a k (p t) r -> p (a k) (t r)", t=2)
    u_v = u.rearrange("a k (c p j) r -> (a k) p c (j r)", c=4, j=2)
    w_v = W_out.rearrange("(c p j) k -> c p (j k)", c=4, j=2)
    o_v = out.rearrange("a k (p t) o -> (a k) p t o", t=2)
    b_v = b.rearrange("a x y o -> (x y) a o")
    bo_v = b_out.rearrange("(x o) -> x o", x=1)

    with ExitStack() as ctx:
        const = ctx.enter_context(tc.tile_pool(name="const", bufs=1))
        hpool = ctx.enter_context(tc.tile_pool(name="hpool", bufs=8))
        upool = ctx.enter_context(tc.tile_pool(name="upool", bufs=8))
        work = ctx.enter_context(tc.tile_pool(name="work", bufs=3))
        prep = ctx.enter_context(tc.tile_pool(name="prep", bufs=PRE_BUFS))
        stg = ctx.enter_context(tc.tile_pool(name="stg", bufs=6))
        psum = ctx.enter_context(tc.psum_pool(name="psum", bufs=8))
        if MANUAL:
            ctx.enter_context(tc.manual_schedule())

        def bank(shape, dtype, name):
            return psum.tile(shape, dtype, name=name, tag="ps")

        ident_f = const.tile([P, P], F32, name="ident_f")
        ident_b = const.tile([P, P], BF16, name="ident_b")
        make_identity(nc, ident_b[:])
        make_identity(nc, ident_f[:])
        ones = const.tile([P, P], BF16, name="ones")
        nc.vector.memset(ones[:], 1.0)
        bias_in = const.tile([P, 2, 1024], BF16, name="bias_in")
        nc.vector.memset(bias_in[:], 0.0)
        c128 = const.tile([P, P], BF16, name="c128")
        nc.vector.memset(c128[:], 128.0)
        bias_pm = const.tile([P, 2048], BF16, name="bias_pm")
        warm = const.tile([P, 1], F32, name="warm")
        nc.vector.memset(warm[:], 0.0)
        nc.scalar.activation(out=warm[:], in_=warm[:], func=ACTF.Gelu)
        nc.scalar.dma_start(out=bias_in[1:2, :, :], in_=b_v)
        for a in range(2):
            nc.scalar.dma_start(out=bias_in[0:1, a, :], in_=bo_v)

        nc.vector.tensor_copy(out=bias_pm[:].rearrange("q (m j p) -> q m j p", m=8, j=2),
                              in_=bias_in[:].rearrange("q a (c p j) -> q (a c) j p", c=4, j=2))

        z_sb = [const.tile([P, 4, 256], BF16, name="z_sb%d" % k) for k in range(4)]
        zT = [const.tile([P, 1024], BF16, name="zT%d" % k) for k in range(4)]
        w_sb = [const.tile([P, 2048], BF16, name="w_sb%d" % c) for c in range(4)]
        gW = [const.tile([P, 4096], BF16, name="gW%d" % n, align_bytes=64) for n in range(2)]
        cW = [const.tile([P, 1024], U32, name="cW%d" % n, align_bytes=64) for n in range(2)]
        sW = [const.tile([P, 1024], U8, name="sW%d" % n, align_bytes=64) for n in range(2)]
        bias_sb = [const.tile([P, 1024], F32, name="bias_sb%d" % a) for a in range(2)]

        h_sb, u_sb, hq, ch, sh, uT, pre, lo_ps, mx_ps, h_ps, u_ps = {}, {}, {}, {}, {}, {}, {}, {}, {}, {}, {}

        def load_z(k):
            nc.sync.dma_start(out=z_sb[k][:], in_=z_v[:, 4 * k : 4 * k + 4, :])

        def load_w(c):
            nc.sync.dma_start(out=w_sb[c][:], in_=w_v[c])

        def load_u(i):
            u_sb[i] = upool.tile([P, 4, 256], BF16, name="u_sb_%d" % i, tag="u")
            nc.sync.dma_start(out=u_sb[i][:], in_=u_v[i])

        def load_h(i):
            h_sb[i] = hpool.tile([P, 2048], BF16, name="h_sb_%d" % i, tag="h")
            nc.sync.dma_start(out=h_sb[i][:], in_=h_v[i])

        def copy_on(eng, out_, in_):
            if eng == "act":
                nc.scalar.copy(out=out_, in_=in_)
            else:
                nc.vector.tensor_copy(out=out_, in_=in_)

        def t_z(k):
            ps = bank([P, 1024], BF16, "z_ps%d" % k)
            for q in range(8):
                nc.tensor.transpose(ps[:, q * P : (q + 1) * P], z_sb[k][:, q // 2, (q % 2) * P : (q % 2 + 1) * P], ident_b[:])
            return ps

        def x_z(k, ps, eng):
            copy_on(eng, zT[k][:], ps[:])

        def t_u(i, half):
            if half == 0:
                u_ps[i] = bank([P, 1024], BF16, "u_ps%d" % i)
            ps = u_ps[i]
            for q in range(4 * half, 4 * half + 4):
                nc.tensor.transpose(ps[:, q * P : (q + 1) * P], u_sb[i][:, q // 2, (q % 2) * P : (q % 2 + 1) * P], ident_b[:])

        def x_u(i, eng):
            uT[i] = work.tile([P, 1024], BF16, name="uT_%d" % i, tag="uT", bufs=4)
            copy_on(eng, uT[i][:], u_ps[i][:])

        def words_T(src_f32, base, name):
            ps = bank([P, 512], F32, name)
            for q in range(4):
                nc.tensor.transpose(ps[:, q * P : (q + 1) * P], src_f32[:, base + q * P : base + (q + 1) * P], ident_f[:])
            return ps

        def t_h(i, t):
            h_ps[i, t] = words_T(h_sb[i][:].bitcast(F32), t * 512, "h_ps%d_%d" % (i, t))

        def x_h(i, t, eng):
            if t == 0:
                hq[i] = work.tile([P, 2048], BF16, name="hq_%d" % i, tag="hq", align_bytes=64)
            dst = hq[i][:].bitcast(F32)[:, t * 512 : (t + 1) * 512].rearrange("q (g f e) -> q g f e", g=2, e=2)
            copy_on(eng, dst, h_ps[i, t][:].rearrange("q (g e f) -> q g f e", g=2, e=2))

        def q_h(i):
            ch[i] = work.tile([P, 512], U32, name="ch_%d" % i, tag="ch", align_bytes=64)
            sh[i] = work.tile([P, 512], U8, name="sh_%d" % i, tag="sh", align_bytes=64)
            nc.vector.quantize_mx(out=ch[i][:].bitcast(FP8X4), scales=sh[i][:], in_=hq[i][:])

        def t_w(c, j):
            return words_T(w_sb[c][:].bitcast(F32), j * 512, "w_ps%d_%d" % (c, j))

        def x_w(c, j, ps, eng):
            off = (c % 2) * 256 + j * P
            dst = gW[c // 2][:].bitcast(F32).rearrange("q (g o e) -> q g o e", g=2, e=2)[:, :, off : off + P, :]
            copy_on(eng, dst, ps[:].rearrange("q (g e o) -> q g o e", g=2, e=2))

        def q_w(n):
            nc.vector.quantize_mx(out=cW[n][:].bitcast(FP8X4), scales=sW[n][:], in_=gW[n][:])

        def bias_mm(a, n):
            ps = bank([P, 512], F32, "b_ps%d_%d" % (a, n))
            nc.tensor.matmul(out=ps[:], lhsT=ones[:], rhs=bias_in[:, a, n * 512 : (n + 1) * 512], start=True, stop=True)
            return ps

        def bias_x(a, n, ps, eng):
            dst = bias_sb[a][:, n * 512 : (n + 1) * 512].rearrange("q (c j p) -> q c j p", c=2, j=2)
            copy_on(eng, dst, ps[:].rearrange("q (c p j) -> q c j p", c=2, j=2))

        def lo(i, t, n):
            ps = bank([P, 512], F32, "lo_ps%d_%d_%d" % (i, t, n))
            q = (i % 4) * 2 + t
            nc.tensor.matmul(out=ps[:], lhsT=zT[i // 4][:, q * P : (q + 1) * P], rhs=uT[i][:, n * 512 : (n + 1) * 512],
                             start=True, stop=p1_engine(i, 2 * t + n) != "act")
            lo_ps[i, t, n] = ps

        def lo_bias(i, t, n):
            m = (i // 8) * 2 + n
            nc.tensor.matmul(out=lo_ps[i, t, n][:], lhsT=c128[:], rhs=bias_pm[:, m * 512 : (m + 1) * 512],
                             start=False, stop=True)

        def p1(i, t, n, eng):
            if (i not in pre):
                pre[i] = prep.tile([P, 2048], F32, name="pre_%d" % i, tag="pre")
            dst = pre[i][:, t * 1024 + n * 512 : t * 1024 + (n + 1) * 512]
            bia = bias_sb[i // 8][:, n * 512 : (n + 1) * 512]
            if eng == "act":
                nc.scalar.activation(out=dst, in_=lo_ps[i, t, n][:], func=ACTF.Copy, scale=1.0 / 128.0)
            else:
                nc.vector.scalar_tensor_tensor(out=dst, in0=lo_ps[i, t, n][:], scalar=1.0 / 128.0, in1=bia,
                                               op0=ALU.mult, op1=ALU.add)

        def mx(i, t, n):
            ps = bank([P, 512], F32, "mx_ps%d_%d_%d" % (i, t, n))
            for g in range(2):
                q = 2 * t + g
                nc.tensor.matmul_mx(out=ps[:], lhsT=ch[i][:, q * P : (q + 1) * P].bitcast(FP8X4),
                                    lhsT_scale=sh[i][:, q * P : (q + 1) * P],
                                    rhs=cW[n][:, g * 512 : (g + 1) * 512].bitcast(FP8X4),
                                    rhs_scale=sW[n][:, g * 512 : (g + 1) * 512], start=(g == 0), stop=(g == 1))
            mx_ps[i, t, n] = ps

        def p2(i, t, n):
            dst = pre[i][:, t * 1024 + n * 512 : t * 1024 + (n + 1) * 512]
            nc.vector.tensor_tensor(out=dst, in0=mx_ps[i, t, n][:], in1=dst, op=ALU.add)

        def ge(i, t):
            st = stg.tile([P, 1024], F32, name="st_%d_%d" % (i, t), tag="st")
            nc.scalar.activation(out=st[:].rearrange("q (c p j) -> q c p j", c=4, j=2),
                                 in_=pre[i][:, t * 1024 : (t + 1) * 1024].rearrange("q (c j p) -> q c p j", c=4, j=2),
                                 func=ACTF.Gelu)
            nc.sync.dma_start(out=o_v[i][:, t, :], in_=st[:])

        def ge_half(i, t, n):
            st = stg.tile([P, 512], F32, name="sth_%d_%d_%d" % (i, t, n), tag="st")
            lo_c = t * 1024 + n * 512
            nc.scalar.activation(out=st[:].rearrange("q (c p j) -> q c p j", c=2, j=2),
                                 in_=pre[i][:, lo_c : lo_c + 512].rearrange("q (c j p) -> q c p j", c=2, j=2),
                                 func=ACTF.Gelu)
            nc.sync.dma_start(out=o_v[i][:, t, n * 512 : (n + 1) * 512], in_=st[:])

        loads = []
        for i in range(UNITS):
            loads.append((i - DU, 1, load_u, i))
            loads.append((i - DH, 2, load_h, i))
        for kk in range(4):
            loads.append((4 * kk - DU, 0, load_z, kk))
        for c in range(4):
            loads.append((W_STEP - 0.5, c, load_w, c))
        loads = sorted(loads, key=lambda e: (e[0], e[1]))
        issued = [0]

        def issue_loads(upto):
            while issued[0] < len(loads) and loads[issued[0]][0] <= upto:
                e = loads[issued[0]]
                e[2](e[3])
                issued[0] += 1

        issue_loads(-DU + LOAD_AHEAD)
        late_ge = None
        for s in range(-DU, UNITS):
            iu, il, ih = s + DU, s + DL, s + DH
            runs = []
            for c in W_AT.get(s, ()):
                for j in range(2):
                    runs.append(("w", c, j))
            if 0 <= ih < UNITS:
                runs.append(("h", ih, 0))
                runs.append(("h", ih, 1))
            if iu % 4 == 0 and iu < UNITS:
                runs.append(("z", iu // 4, 0))
            if iu < UNITS:
                runs.append(("u", iu, 0))
                runs.append(("u", iu, 1))
            if il in (0, 8):
                pb = [bias_mm(il // 8, n) for n in range(2)]
                for n in range(2):
                    bias_x(il // 8, n, pb[n], "dve")
            slots = []
            if 0 <= il < UNITS:
                for j in range(4):
                    slots.append(("lo", j))
                    if p1_engine(il, j) == "act":
                        slots.append(("bias", j))
            gaps = max(len(slots) - 1, 1)
            per_gap = (len(runs) + gaps - 1) // gaps
            done = 0
            for k in range(max(len(slots), 1)):
                if slots:
                    kind, j = slots[k]
                    if kind == "lo":
                        lo(il, j // 2, j % 2)
                    else:
                        lo_bias(il, j // 2, j % 2)
                    if kind == "bias" or p1_engine(il, j) != "act":
                        p1(il, j // 2, j % 2, p1_engine(il, j))
                if k < gaps:
                    todo = runs[done : done + per_gap]
                    done += len(todo)
                    held = []
                    for kind, a, bb in todo:
                        if kind == "w":
                            held.append(t_w(a, bb))
                        elif kind == "h":
                            t_h(a, bb)
                            held.append(None)
                        elif kind == "z":
                            held.append(t_z(a))
                        else:
                            t_u(a, bb)
                            held.append(None)
                    for (kind, a, bb), ps in zip(todo, held):
                        if kind == "w":
                            x_w(a, bb, ps, "act" if bb in XW_ACT else "dve")
                            if bb == 1 and a % 2 == 1:
                                q_w(a // 2)
                        elif kind == "h":
                            x_h(a, bb, "act")
                        elif kind == "z":
                            x_z(a, ps, XU_ENG)
                        elif bb == 1:
                            x_u(a, XU_ENG)
            if late_ge is not None:
                ge(*late_ge)
                late_ge = None
            issue_loads(s + 1 + LOAD_AHEAD)
            for j in range(4):
                t, n = j // 2, j % 2
                if s >= 0:
                    mx(s, t, n)
                    p2(s, t, n)
                    if s == UNITS - 1:
                        ge_half(s, t, n)
                    elif j == 1:
                        ge(s, 0)
            if 0 <= ih < UNITS:
                q_h(ih)
            if 0 <= s < UNITS - 1:
                late_ge = (s, 1)
